import numpy as np
import ml_dtypes


def mxq(x, axis, fmt="e4m3"):
    dtype, down = {"e4m3": (ml_dtypes.float8_e4m3fn, 7), "e5m2": (ml_dtypes.float8_e5m2, 14)}[fmt]
    v = np.moveaxis(np.asarray(x, np.float32).astype(ml_dtypes.bfloat16).astype(np.float64), axis, -1)
    blocks = v.reshape(v.shape[:-1] + (-1, 32))
    amax = np.abs(blocks).max(-1, keepdims=True)
    byte = np.maximum(np.where(amax > 0, np.frexp(amax)[1] - 1 + 127, 0) - down, 1)
    scale = np.exp2(byte - 127.0)
    codes = (blocks / scale).astype(np.float32).astype(dtype).astype(np.float64)
    return np.moveaxis((codes * scale).reshape(v.shape), -1, axis)


WIDE = False


def mx_kscale(k):
    if not WIDE:
        return np.ones(k)
    levels = np.array([10, -10, 5, -5, 0])
    a = np.random.permutation(np.resize(levels, k // 512 * 4)).reshape(k // 512, 4)
    idx = np.arange(k)
    return np.exp2(a[idx // 512, idx % 128 // 32])


BF16 = ml_dtypes.bfloat16


def bf(x):
    return np.asarray(x, np.float32).astype(BF16)


def f64(x):
    return np.asarray(x).astype(np.float64)


B, T, HP, WP, NH, D, DFF = 16, 8, 3, 4, 16, 1024, 4096
HW = HP * WP


def setup_inputs():
    s = mx_kscale(D)
    c = np.random.standard_normal((B * T, 1 + HW, D)) * 1.5 / np.sqrt(1 + HW)
    c[:, 0, :] *= 5.0
    return {"ctx_s": bf(c * s),
            "x_res": bf(np.random.standard_normal((B, 1 + HW * T, D)) * 1.1),
            "s_out_w": bf(np.random.standard_normal((D, D)) / np.sqrt(D) / s[:, None]),
            "s_out_b": bf(0.1 * np.random.standard_normal(D))}


def reference(ctx_s, x_res, s_out_w, s_out_b):
    res_s = (mxq(f64(ctx_s), 2, "e4m3") @ mxq(f64(s_out_w), 0, "e4m3")) + f64(s_out_b)
    cls_tok = res_s[:, 0, :].reshape(B, T, D).mean(axis=1, keepdims=True)
    res_p = res_s[:, 1:, :].reshape(B, T, HW, D).swapaxes(1, 2).reshape(B, HW * T, D)
    return f64(x_res) + np.concatenate([cls_tok, res_p], axis=1)

@@ -1,0 +1,253 @@
+from contextlib import ExitStack
+
+import concourse.mybir as mybir
+from concourse.masks import make_identity
+
+F32 = mybir.dt.float32
+BF16 = mybir.dt.bfloat16
+I32 = mybir.dt.int32
+U32 = mybir.dt.uint32
+U8 = mybir.dt.uint8
+FP8X4 = mybir.dt.float8_e4m3fn_x4
+ADD = mybir.AluOpType.add
+MULT = mybir.AluOpType.mult
+
+P = 128
+SAMPLES = 16
+FRAMES = 8
+PATCHES = 12
+TOKENS = 1 + PATCHES
+D = 1024
+K_PASS = 512
+PASSES = D // K_PASS
+BANK = 512
+HALVES = D // BANK
+WORDS = D // 2
+BLOCKS = WORDS // P
+CHUNK = 2
+RUN = 4
+W_VECTOR_COLS = 336
+VECTOR_EVERY = 4
+
+FLOPS = 2 * P * TOKENS * D * D
+
+
+def tile_timesformerlayer_pc_kernel(tc, ctx_s, x_res, s_out_w, s_out_b, out):
+    nc = tc.nc
+    token_groups = [[0], [1]] + [[j, j + 1] for j in range(2, TOKENS - 1, 2)] + [[TOKENS - 1]]
+
+    with ExitStack() as stack:
+        keep = stack.enter_context(tc.tile_pool(name="keep", bufs=1))
+        work = stack.enter_context(tc.tile_pool(name="work", bufs=3))
+        psum_turn = stack.enter_context(tc.psum_pool(name="psum_turn", bufs=2))
+        psum_acc = stack.enter_context(tc.psum_pool(name="psum_acc", bufs=6))
+
+        ident = keep.tile([P, P], F32)
+        ones = keep.tile([P, P], BF16)
+        bias_rows = keep.tile([P, D], BF16)
+        bias_all = keep.tile([P, D], F32)
+        ctx_chunks = [
+            keep.tile([P, min(CHUNK, TOKENS - first) * D], BF16, name="ctx%d" % first)
+            for first in range(0, TOKENS, CHUNK)
+        ]
+        w_raw = [keep.tile([P, 4, D], BF16, name="w_raw%d" % g) for g in range(PASSES)]
+        w_grouped = [
+            keep.tile([P, D, 4], BF16, name="w_grouped%d" % g, align_bytes=64) for g in range(PASSES)
+        ]
+        w_codes = [keep.tile([P, D], U32, name="w_codes%d" % g, align_bytes=64) for g in range(PASSES)]
+        w_scales = [keep.tile([P, D], U8, name="w_scales%d" % g, align_bytes=64) for g in range(PASSES)]
+        x_patch = [keep.tile([P, D], BF16, name="x_patch%d" % p) for p in range(PATCHES)]
+        y_patch = [keep.tile([P, D], F32, name="y_patch%d" % p) for p in range(PATCHES)]
+        x_class = keep.tile([P, P], BF16)
+        bias_class = keep.tile([P, P], BF16)
+        y_class = keep.tile([P, P], F32)
+        class_sums = keep.tile([P, P], F32)
+
+        def patch_rows(dram, p):
+            return dram[:, 1 + p * FRAMES : 1 + (p + 1) * FRAMES, :]
+
+        def class_rows(dram):
+            return dram[:, 0, :].rearrange("b (c n) -> c b n", n=P)
+
+        make_identity(nc, ident[:])
+        nc.vector.memset(ones[:], 1.0)
+        nc.vector.memset(bias_rows[:].bitcast(I32), 0)
+
+        def load_ctx(c):
+            first = c * CHUNK
+            last = min(first + CHUNK, TOKENS)
+            nc.sync.dma_start(
+                out=ctx_chunks[c][:], in_=ctx_s[:, first:last, :].rearrange("s j d -> s (j d)")
+            )
+
+        def load_w(g):
+            rows = s_out_w[g * K_PASS : (g + 1) * K_PASS, :]
+            nc.sync.dma_start(
+                out=w_raw[g][:].rearrange("p (u e) n -> p u (e n)", e=2),
+                in_=rows.rearrange("(u p e) n -> p u (e n)", u=2, e=2),
+            )
+
+        nc.sync.dma_start(out=bias_rows[0:1, :], in_=s_out_b.rearrange("(o n) -> o n", o=1))
+        load_ctx(0)
+        load_w(0)
+        load_w(1)
+        nc.sync.dma_start(out=x_class[:], in_=class_rows(x_res))
+        nc.sync.dma_start(
+            out=bias_class[:],
+            in_=s_out_b.rearrange("(c o n) -> c o n", o=1, n=P).to_broadcast([D // P, SAMPLES, P]),
+        )
+        nc.sync.dma_start(out=x_patch[0][:], in_=patch_rows(x_res, 0))
+        for c in range(1, len(ctx_chunks)):
+            load_ctx(c)
+            for j in range(c * CHUNK, min((c + 1) * CHUNK, TOKENS)):
+                nc.sync.dma_start(out=x_patch[j - 1][:], in_=patch_rows(x_res, j - 1))
+
+        for h in range(HALVES):
+            spread = psum_acc.tile([P, BANK], F32, tag="acc")
+            nc.tensor.matmul(
+                out=spread[:], lhsT=ones[:], rhs=bias_rows[:, h * BANK : (h + 1) * BANK], start=True, stop=True
+            )
+            nc.scalar.copy(out=bias_all[:, h * BANK : (h + 1) * BANK], in_=spread[:])
+
+        def add_bias(tokens):
+            for j in tokens:
+                if j == 0:
+                    nc.gpsimd.tensor_tensor(out=y_class[:], in0=x_class[:], in1=bias_class[:], op=ADD)
+                else:
+                    p = j - 1
+                    engine = nc.vector if p % VECTOR_EVERY == VECTOR_EVERY - 1 else nc.gpsimd
+                    engine.tensor_tensor(out=y_patch[p][:], in0=x_patch[p][:], in1=bias_all[:], op=ADD)
+
+        def turn(tokens):
+            grouped = work.tile([P, len(tokens) * D], BF16, align_bytes=64, tag="grouped")
+            grouped_words = grouped[:].bitcast(F32)
+            for i, j in enumerate(tokens):
+                words = ctx_chunks[j // CHUNK][:].bitcast(F32)
+                turned = psum_turn.tile([P, BLOCKS, P], F32, tag="turned")
+                for blk in range(BLOCKS):
+                    first = (j % CHUNK) * WORDS + blk * P
+                    nc.tensor.transpose(out=turned[:, blk, :], in_=words[:, first : first + P], identity=ident[:])
+                nc.scalar.copy(
+                    out=grouped_words[:, i * WORDS : (i + 1) * WORDS].rearrange(
+                        "p (g r u) -> p g r u", g=PASSES, u=2
+                    ),
+                    in_=turned[:].rearrange("p (g u) r -> p g r u", u=2),
+                )
+            return grouped
+
+        def quantise(tokens, grouped):
+            codes = work.tile([P, len(tokens) * PASSES * P], U32, align_bytes=64, tag="codes")
+            scales = work.tile([P, len(tokens) * PASSES * P], U8, align_bytes=64, tag="scales")
+            nc.vector.quantize_mx(out=codes[:].bitcast(FP8X4), scales=scales[:], in_=grouped[:])
+            return codes, scales
+
+        def regroup_w(copy, g, first, last):
+            copy(
+                out=w_grouped[g][:, first:last, :].rearrange("p (c i) t -> p c t i", i=RUN),
+                in_=w_raw[g][:, :, first:last].rearrange("p t (c i) -> p c t i", i=RUN),
+            )
+
+        def prepare_w(g):
+            for h in range(HALVES):
+                regroup_w(nc.vector.tensor_copy, g, h * BANK, h * BANK + W_VECTOR_COLS)
+                regroup_w(nc.scalar.copy, g, h * BANK + W_VECTOR_COLS, (h + 1) * BANK)
+            for h in range(HALVES):
+                cols = slice(h * BANK, (h + 1) * BANK)
+                nc.vector.quantize_mx(
+                    out=w_codes[g][:, cols].bitcast(FP8X4),
+                    scales=w_scales[g][:, cols],
+                    in_=w_grouped[g][:, cols, :].rearrange("p n t -> p (n t)"),
+                )
+
+        def multiply_patch(codes, scales, i):
+            banks = []
+            for h in range(HALVES):
+                acc = psum_acc.tile([P, BANK], F32, tag="acc")
+                for g in range(PASSES):
+                    rows = slice((i * PASSES + g) * P, (i * PASSES + g + 1) * P)
+                    cols = slice(h * BANK, (h + 1) * BANK)
+                    nc.tensor.matmul_mx(
+                        out=acc[:],
+                        lhsT=codes[:, rows].bitcast(FP8X4),
+                        lhsT_scale=scales[:, rows],
+                        rhs=w_codes[g][:, cols].bitcast(FP8X4),
+                        rhs_scale=w_scales[g][:, cols],
+                        start=(g == 0),
+                        stop=(g == PASSES - 1),
+                    )
+                banks.append(acc)
+            return banks
+
+        def finish_patch(p, banks):
+            for h in range(HALVES):
+                cols = slice(h * BANK, (h + 1) * BANK)
+                nc.vector.tensor_tensor(out=y_patch[p][:, cols], in0=banks[h][:], in1=y_patch[p][:, cols], op=ADD)
+            nc.sync.dma_start(out=patch_rows(out, p), in_=y_patch[p][:])
+
+        def multiply_class(codes, scales, i):
+            banks = []
+            for h in range(HALVES):
+                acc = psum_acc.tile([P, BANK], F32, tag="acc")
+                for q in range(BANK // P):
+                    cols = slice(h * BANK + q * P, h * BANK + (q + 1) * P)
+                    for g in range(PASSES):
+                        rows = slice((i * PASSES + g) * P, (i * PASSES + g + 1) * P)
+                        nc.tensor.matmul_mx(
+                            out=acc[:, q * P : (q + 1) * P],
+                            lhsT=w_codes[g][:, cols].bitcast(FP8X4),
+                            lhsT_scale=w_scales[g][:, cols],
+                            rhs=codes[:, rows].bitcast(FP8X4),
+                            rhs_scale=scales[:, rows],
+                            start=(g == 0),
+                            stop=(g == PASSES - 1),
+                        )
+                banks.append(acc)
+            return banks
+
+        def finish_class(banks):
+            per_bank = BANK // FRAMES
+            for h in range(HALVES):
+                nc.vector.tensor_reduce(
+                    out=class_sums[:, h * per_bank : (h + 1) * per_bank],
+                    in_=banks[h][:].rearrange("p (cb t) -> p cb t", t=FRAMES),
+                    axis=mybir.AxisListType.X,
+                    op=ADD,
+                )
+            back = psum_turn.tile([P, BLOCKS, P], F32, tag="turned")
+            nc.tensor.transpose(out=back[:, 0, :], in_=class_sums[:], identity=ident[:])
+            nc.vector.scalar_tensor_tensor(
+                out=y_class[:], in0=back[:, 0, :], scalar=1.0 / FRAMES, in1=y_class[:], op0=MULT, op1=ADD
+            )
+            nc.sync.dma_start(out=class_rows(out), in_=y_class[:])
+
+        def multiply(tokens, codes, scales):
+            return [
+                multiply_class(codes, scales, i) if j == 0 else multiply_patch(codes, scales, i)
+                for i, j in enumerate(tokens)
+            ]
+
+        def finish(tokens, banks):
+            for i, j in enumerate(tokens):
+                if j == 0:
+                    finish_class(banks[i])
+                else:
+                    finish_patch(j - 1, banks[i])
+
+        n_groups = len(token_groups)
+        quantised = {}
+        for u in range(2):
+            quantised[u] = quantise(token_groups[u], turn(token_groups[u]))
+        for g in range(PASSES):
+            prepare_w(g)
+        for u in range(3):
+            add_bias(token_groups[u])
+        for u in range(n_groups):
+            codes, scales = quantised[u]
+            banks = multiply(token_groups[u], codes, scales)
+            if u + 2 < n_groups:
+                grouped = turn(token_groups[u + 2])
+            if u + 3 < n_groups:
+                add_bias(token_groups[u + 3])
+            finish(token_groups[u], banks)
+            if u + 2 < n_groups:
+                quantised[u + 2] = quantise(token_groups[u + 2], grouped)

@@ -41,6 +41,7 @@ def tile_timesformerlayer_pc_kernel(tc, ctx_s, x_res, s_out_w, s_out_b, out):
         work = stack.enter_context(tc.tile_pool(name="work", bufs=3))
         psum_turn = stack.enter_context(tc.psum_pool(name="psum_turn", bufs=2))
         psum_acc = stack.enter_context(tc.psum_pool(name="psum_acc", bufs=6))
+        stack.enter_context(tc.manual_schedule())
 
         ident = keep.tile([P, P], F32)
         ones = keep.tile([P, P], BF16)

@@ -27,7 +27,6 @@ BLOCKS = WORDS // P
 CHUNK = 2
 RUN = 4
 W_VECTOR_COLS = 336
-VECTOR_EVERY = 4
 
 FLOPS = 2 * P * TOKENS * D * D
 
@@ -113,11 +112,10 @@ def tile_timesformerlayer_pc_kernel(tc, ctx_s, x_res, s_out_w, s_out_b, out):
         def add_bias(tokens):
             for j in tokens:
                 if j == 0:
-                    nc.gpsimd.tensor_tensor(out=y_class[:], in0=x_class[:], in1=bias_class[:], op=ADD)
+                    nc.vector.tensor_tensor(out=y_class[:], in0=x_class[:], in1=bias_class[:], op=ADD)
                 else:
                     p = j - 1
-                    engine = nc.vector if p % VECTOR_EVERY == VECTOR_EVERY - 1 else nc.gpsimd
-                    engine.tensor_tensor(out=y_patch[p][:], in0=x_patch[p][:], in1=bias_all[:], op=ADD)
+                    nc.vector.tensor_tensor(out=y_patch[p][:], in0=x_patch[p][:], in1=bias_all[:], op=ADD)
 
         def turn(tokens):
             grouped = work.tile([P, len(tokens) * D], BF16, align_bytes=64, tag="grouped")

@@ -26,7 +26,8 @@ WORDS = D // 2
 BLOCKS = WORDS // P
 CHUNK = 2
 RUN = 4
-W_VECTOR_COLS = 336
+W_VECTOR_COLS = 256
+VECTOR_EVERY = 3
 
 FLOPS = 2 * P * TOKENS * D * D
 
@@ -34,18 +35,21 @@ FLOPS = 2 * P * TOKENS * D * D
 def tile_timesformerlayer_pc_kernel(tc, ctx_s, x_res, s_out_w, s_out_b, out):
     nc = tc.nc
     token_groups = [[0], [1]] + [[j, j + 1] for j in range(2, TOKENS - 1, 2)] + [[TOKENS - 1]]
+    halves = [slice(h * BANK, (h + 1) * BANK) for h in range(HALVES)]
 
     with ExitStack() as stack:
         keep = stack.enter_context(tc.tile_pool(name="keep", bufs=1))
         work = stack.enter_context(tc.tile_pool(name="work", bufs=3))
+        psum_bias = stack.enter_context(tc.psum_pool(name="psum_bias", bufs=1))
         psum_turn = stack.enter_context(tc.psum_pool(name="psum_turn", bufs=2))
-        psum_acc = stack.enter_context(tc.psum_pool(name="psum_acc", bufs=6))
+        psum_acc = stack.enter_context(tc.psum_pool(name="psum_acc", bufs=4))
         stack.enter_context(tc.manual_schedule())
 
         ident = keep.tile([P, P], F32)
         ones = keep.tile([P, P], BF16)
         bias_rows = keep.tile([P, D], BF16)
-        bias_all = keep.tile([P, D], F32)
+        bias_sbuf = keep.tile([P, D], F32)
+        bias_psum = [psum_bias.tile([P, BANK], F32, name="bias_psum%d" % h) for h in range(HALVES)]
         ctx_chunks = [
             keep.tile([P, min(CHUNK, TOKENS - first) * D], BF16, name="ctx%d" % first)
             for first in range(0, TOKENS, CHUNK)
@@ -69,9 +73,9 @@ def tile_timesformerlayer_pc_kernel(tc, ctx_s, x_res, s_out_w, s_out_b, out):
         def class_rows(dram):
             return dram[:, 0, :].rearrange("b (c n) -> c b n", n=P)
 
-        make_identity(nc, ident[:])
-        nc.vector.memset(ones[:], 1.0)
         nc.vector.memset(bias_rows[:].bitcast(I32), 0)
+        nc.vector.memset(ones[:], 1.0)
+        make_identity(nc, ident[:])
 
         def load_ctx(c):
             first = c * CHUNK
@@ -87,35 +91,49 @@ def tile_timesformerlayer_pc_kernel(tc, ctx_s, x_res, s_out_w, s_out_b, out):
                 in_=rows.rearrange("(u p e) n -> p u (e n)", u=2, e=2),
             )
 
-        nc.sync.dma_start(out=bias_rows[0:1, :], in_=s_out_b.rearrange("(o n) -> o n", o=1))
-        load_ctx(0)
+        def load_x(p):
+            nc.sync.dma_start(out=x_patch[p][:], in_=patch_rows(x_res, p))
+
+        nc.scalar.dma_start(out=bias_rows[0:1, :], in_=s_out_b.rearrange("(o n) -> o n", o=1))
         load_w(0)
+        load_x(0)
         load_w(1)
+        load_ctx(0)
+        load_x(1)
         nc.sync.dma_start(out=x_class[:], in_=class_rows(x_res))
         nc.sync.dma_start(
             out=bias_class[:],
             in_=s_out_b.rearrange("(c o n) -> c o n", o=1, n=P).to_broadcast([D // P, SAMPLES, P]),
         )
-        nc.sync.dma_start(out=x_patch[0][:], in_=patch_rows(x_res, 0))
         for c in range(1, len(ctx_chunks)):
             load_ctx(c)
-            for j in range(c * CHUNK, min((c + 1) * CHUNK, TOKENS)):
-                nc.sync.dma_start(out=x_patch[j - 1][:], in_=patch_rows(x_res, j - 1))
+            for p in range(c * CHUNK, min((c + 1) * CHUNK, PATCHES)):
+                load_x(p)
 
         for h in range(HALVES):
             spread = psum_acc.tile([P, BANK], F32, tag="acc")
-            nc.tensor.matmul(
-                out=spread[:], lhsT=ones[:], rhs=bias_rows[:, h * BANK : (h + 1) * BANK], start=True, stop=True
-            )
-            nc.scalar.copy(out=bias_all[:, h * BANK : (h + 1) * BANK], in_=spread[:])
+            for target in (spread, bias_psum[h]):
+                nc.tensor.matmul(out=target[:], lhsT=ones[:], rhs=bias_rows[:, halves[h]], start=True, stop=True)
+            nc.scalar.copy(out=bias_sbuf[:, halves[h]], in_=spread[:])
 
         def add_bias(tokens):
             for j in tokens:
+                p = j - 1
                 if j == 0:
                     nc.vector.tensor_tensor(out=y_class[:], in0=x_class[:], in1=bias_class[:], op=ADD)
+                elif p % VECTOR_EVERY == VECTOR_EVERY - 1:
+                    for h in range(HALVES):
+                        nc.vector.tensor_tensor(
+                            out=y_patch[p][:, halves[h]], in0=bias_psum[h][:], in1=x_patch[p][:, halves[h]], op=ADD
+                        )
                 else:
-                    p = j - 1
-                    nc.vector.tensor_tensor(out=y_patch[p][:], in0=x_patch[p][:], in1=bias_all[:], op=ADD)
+                    for h in range(HALVES):
+                        nc.gpsimd.tensor_tensor(
+                            out=y_patch[p][:, halves[h]],
+                            in0=x_patch[p][:, halves[h]],
+                            in1=bias_sbuf[:, halves[h]],
+                            op=ADD,
+                        )
 
         def turn(tokens):
             grouped = work.tile([P, len(tokens) * D], BF16, align_bytes=64, tag="grouped")
@@ -151,11 +169,10 @@ def tile_timesformerlayer_pc_kernel(tc, ctx_s, x_res, s_out_w, s_out_b, out):
                 regroup_w(nc.vector.tensor_copy, g, h * BANK, h * BANK + W_VECTOR_COLS)
                 regroup_w(nc.scalar.copy, g, h * BANK + W_VECTOR_COLS, (h + 1) * BANK)
             for h in range(HALVES):
-                cols = slice(h * BANK, (h + 1) * BANK)
                 nc.vector.quantize_mx(
-                    out=w_codes[g][:, cols].bitcast(FP8X4),
-                    scales=w_scales[g][:, cols],
-                    in_=w_grouped[g][:, cols, :].rearrange("p n t -> p (n t)"),
+                    out=w_codes[g][:, halves[h]].bitcast(FP8X4),
+                    scales=w_scales[g][:, halves[h]],
+                    in_=w_grouped[g][:, halves[h], :].rearrange("p n t -> p (n t)"),
                 )
 
         def multiply_patch(codes, scales, i):
@@ -164,13 +181,12 @@ def tile_timesformerlayer_pc_kernel(tc, ctx_s, x_res, s_out_w, s_out_b, out):
                 acc = psum_acc.tile([P, BANK], F32, tag="acc")
                 for g in range(PASSES):
                     rows = slice((i * PASSES + g) * P, (i * PASSES + g + 1) * P)
-                    cols = slice(h * BANK, (h + 1) * BANK)
                     nc.tensor.matmul_mx(
                         out=acc[:],
                         lhsT=codes[:, rows].bitcast(FP8X4),
                         lhsT_scale=scales[:, rows],
-                        rhs=w_codes[g][:, cols].bitcast(FP8X4),
-                        rhs_scale=w_scales[g][:, cols],
+                        rhs=w_codes[g][:, halves[h]].bitcast(FP8X4),
+                        rhs_scale=w_scales[g][:, halves[h]],
                         start=(g == 0),
                         stop=(g == PASSES - 1),
                     )
@@ -179,9 +195,10 @@ def tile_timesformerlayer_pc_kernel(tc, ctx_s, x_res, s_out_w, s_out_b, out):
 
         def finish_patch(p, banks):
             for h in range(HALVES):
-                cols = slice(h * BANK, (h + 1) * BANK)
-                nc.vector.tensor_tensor(out=y_patch[p][:, cols], in0=banks[h][:], in1=y_patch[p][:, cols], op=ADD)
-            nc.sync.dma_start(out=patch_rows(out, p), in_=y_patch[p][:])
+                nc.vector.tensor_tensor(
+                    out=y_patch[p][:, halves[h]], in0=banks[h][:], in1=y_patch[p][:, halves[h]], op=ADD
+                )
+                nc.sync.dma_start(out=patch_rows(out, p)[:, :, halves[h]], in_=y_patch[p][:, halves[h]])
 
         def multiply_class(codes, scales, i):
             banks = []
@@ -233,20 +250,18 @@ def tile_timesformerlayer_pc_kernel(tc, ctx_s, x_res, s_out_w, s_out_b, out):
                     finish_patch(j - 1, banks[i])
 
         n_groups = len(token_groups)
+        for g in range(PASSES):
+            prepare_w(g)
         quantised = {}
         for u in range(2):
             quantised[u] = quantise(token_groups[u], turn(token_groups[u]))
-        for g in range(PASSES):
-            prepare_w(g)
-        for u in range(3):
             add_bias(token_groups[u])
         for u in range(n_groups):
             codes, scales = quantised[u]
             banks = multiply(token_groups[u], codes, scales)
             if u + 2 < n_groups:
                 grouped = turn(token_groups[u + 2])
-            if u + 3 < n_groups:
-                add_bias(token_groups[u + 3])
+                add_bias(token_groups[u + 2])
             finish(token_groups[u], banks)
             if u + 2 < n_groups:
                 quantised[u + 2] = quantise(token_groups[u + 2], grouped)

@@ -27,7 +27,7 @@ BLOCKS = WORDS // P
 CHUNK = 2
 RUN = 4
 W_VECTOR_COLS = 256
-VECTOR_EVERY = 3
+VECTOR_EVERY = 2
 
 FLOPS = 2 * P * TOKENS * D * D
 
@@ -47,6 +47,7 @@ def tile_timesformerlayer_pc_kernel(tc, ctx_s, x_res, s_out_w, s_out_b, out):
 
         ident = keep.tile([P, P], F32)
         ones = keep.tile([P, P], BF16)
+        bias_row = keep.tile([1, D], BF16)
         bias_rows = keep.tile([P, D], BF16)
         bias_sbuf = keep.tile([P, D], F32)
         bias_psum = [psum_bias.tile([P, BANK], F32, name="bias_psum%d" % h) for h in range(HALVES)]
@@ -94,7 +95,7 @@ def tile_timesformerlayer_pc_kernel(tc, ctx_s, x_res, s_out_w, s_out_b, out):
         def load_x(p):
             nc.sync.dma_start(out=x_patch[p][:], in_=patch_rows(x_res, p))
 
-        nc.scalar.dma_start(out=bias_rows[0:1, :], in_=s_out_b.rearrange("(o n) -> o n", o=1))
+        nc.sync.dma_start(out=bias_row[:], in_=s_out_b.rearrange("(o n) -> o n", o=1))
         load_w(0)
         load_x(0)
         load_w(1)
@@ -110,6 +111,7 @@ def tile_timesformerlayer_pc_kernel(tc, ctx_s, x_res, s_out_w, s_out_b, out):
             for p in range(c * CHUNK, min((c + 1) * CHUNK, PATCHES)):
                 load_x(p)
 
+        nc.vector.tensor_copy(out=bias_rows[0:1, :], in_=bias_row[:])
         for h in range(HALVES):
             spread = psum_acc.tile([P, BANK], F32, tag="acc")
             for target in (spread, bias_psum[h]):

@@ -27,7 +27,6 @@ BLOCKS = WORDS // P
 CHUNK = 2
 RUN = 4
 W_VECTOR_COLS = 256
-VECTOR_EVERY = 2
 
 FLOPS = 2 * P * TOKENS * D * D
 
@@ -40,17 +39,16 @@ def tile_timesformerlayer_pc_kernel(tc, ctx_s, x_res, s_out_w, s_out_b, out):
     with ExitStack() as stack:
         keep = stack.enter_context(tc.tile_pool(name="keep", bufs=1))
         work = stack.enter_context(tc.tile_pool(name="work", bufs=3))
-        psum_bias = stack.enter_context(tc.psum_pool(name="psum_bias", bufs=1))
         psum_turn = stack.enter_context(tc.psum_pool(name="psum_turn", bufs=2))
-        psum_acc = stack.enter_context(tc.psum_pool(name="psum_acc", bufs=4))
+        psum_acc = stack.enter_context(tc.psum_pool(name="psum_acc", bufs=6))
         stack.enter_context(tc.manual_schedule())
 
         ident = keep.tile([P, P], F32)
+        ident_bf16 = keep.tile([P, P], BF16)
         ones = keep.tile([P, P], BF16)
         bias_row = keep.tile([1, D], BF16)
         bias_rows = keep.tile([P, D], BF16)
-        bias_sbuf = keep.tile([P, D], F32)
-        bias_psum = [psum_bias.tile([P, BANK], F32, name="bias_psum%d" % h) for h in range(HALVES)]
+        bias_all = keep.tile([P, D], F32)
         ctx_chunks = [
             keep.tile([P, min(CHUNK, TOKENS - first) * D], BF16, name="ctx%d" % first)
             for first in range(0, TOKENS, CHUNK)
@@ -77,6 +75,7 @@ def tile_timesformerlayer_pc_kernel(tc, ctx_s, x_res, s_out_w, s_out_b, out):
         nc.vector.memset(bias_rows[:].bitcast(I32), 0)
         nc.vector.memset(ones[:], 1.0)
         make_identity(nc, ident[:])
+        make_identity(nc, ident_bf16[:])
 
         def load_ctx(c):
             first = c * CHUNK
@@ -114,28 +113,27 @@ def tile_timesformerlayer_pc_kernel(tc, ctx_s, x_res, s_out_w, s_out_b, out):
         nc.vector.tensor_copy(out=bias_rows[0:1, :], in_=bias_row[:])
         for h in range(HALVES):
             spread = psum_acc.tile([P, BANK], F32, tag="acc")
-            for target in (spread, bias_psum[h]):
-                nc.tensor.matmul(out=target[:], lhsT=ones[:], rhs=bias_rows[:, halves[h]], start=True, stop=True)
-            nc.scalar.copy(out=bias_sbuf[:, halves[h]], in_=spread[:])
+            nc.tensor.matmul(out=spread[:], lhsT=ones[:], rhs=bias_rows[:, halves[h]], start=True, stop=True)
+            nc.scalar.copy(out=bias_all[:, halves[h]], in_=spread[:])
 
         def add_bias(tokens):
             for j in tokens:
                 p = j - 1
                 if j == 0:
                     nc.vector.tensor_tensor(out=y_class[:], in0=x_class[:], in1=bias_class[:], op=ADD)
-                elif p % VECTOR_EVERY == VECTOR_EVERY - 1:
+                elif p % 3 == 0:
                     for h in range(HALVES):
-                        nc.vector.tensor_tensor(
-                            out=y_patch[p][:, halves[h]], in0=bias_psum[h][:], in1=x_patch[p][:, halves[h]], op=ADD
+                        summed = psum_acc.tile([P, BANK], F32, tag="acc")
+                        nc.tensor.matmul(
+                            out=summed[:], lhsT=ident_bf16[:], rhs=x_patch[p][:, halves[h]], start=True, stop=False
                         )
+                        nc.tensor.matmul(
+                            out=summed[:], lhsT=ones[:], rhs=bias_rows[:, halves[h]], start=False, stop=True
+                        )
+                        nc.scalar.copy(out=y_patch[p][:, halves[h]], in_=summed[:])
                 else:
-                    for h in range(HALVES):
-                        nc.gpsimd.tensor_tensor(
-                            out=y_patch[p][:, halves[h]],
-                            in0=x_patch[p][:, halves[h]],
-                            in1=bias_sbuf[:, halves[h]],
-                            op=ADD,
-                        )
+                    engine = nc.gpsimd if p % 3 == 1 else nc.vector
+                    engine.tensor_tensor(out=y_patch[p][:], in0=x_patch[p][:], in1=bias_all[:], op=ADD)
 
         def turn(tokens):
             grouped = work.tile([P, len(tokens) * D], BF16, align_bytes=64, tag="grouped")

@@ -24,9 +24,11 @@ BANK = 512
 HALVES = D // BANK
 WORDS = D // 2
 BLOCKS = WORDS // P
+COLUMN_BLOCKS = D // P
 CHUNK = 2
 RUN = 4
 W_VECTOR_COLS = 256
+VECTOR_EVERY = 2
 
 FLOPS = 2 * P * TOKENS * D * D
 
@@ -39,8 +41,9 @@ def tile_timesformerlayer_pc_kernel(tc, ctx_s, x_res, s_out_w, s_out_b, out):
     with ExitStack() as stack:
         keep = stack.enter_context(tc.tile_pool(name="keep", bufs=1))
         work = stack.enter_context(tc.tile_pool(name="work", bufs=3))
+        psum_bias = stack.enter_context(tc.psum_pool(name="psum_bias", bufs=1))
         psum_turn = stack.enter_context(tc.psum_pool(name="psum_turn", bufs=2))
-        psum_acc = stack.enter_context(tc.psum_pool(name="psum_acc", bufs=6))
+        psum_acc = stack.enter_context(tc.psum_pool(name="psum_acc", bufs=4))
         stack.enter_context(tc.manual_schedule())
 
         ident = keep.tile([P, P], F32)
@@ -48,7 +51,8 @@ def tile_timesformerlayer_pc_kernel(tc, ctx_s, x_res, s_out_w, s_out_b, out):
         ones = keep.tile([P, P], BF16)
         bias_row = keep.tile([1, D], BF16)
         bias_rows = keep.tile([P, D], BF16)
-        bias_all = keep.tile([P, D], F32)
+        bias_sbuf = keep.tile([P, D], F32)
+        bias_psum = [psum_bias.tile([P, BANK], F32, name="bias_psum%d" % h) for h in range(HALVES)]
         ctx_chunks = [
             keep.tile([P, min(CHUNK, TOKENS - first) * D], BF16, name="ctx%d" % first)
             for first in range(0, TOKENS, CHUNK)
@@ -61,16 +65,17 @@ def tile_timesformerlayer_pc_kernel(tc, ctx_s, x_res, s_out_w, s_out_b, out):
         w_scales = [keep.tile([P, D], U8, name="w_scales%d" % g, align_bytes=64) for g in range(PASSES)]
         x_patch = [keep.tile([P, D], BF16, name="x_patch%d" % p) for p in range(PATCHES)]
         y_patch = [keep.tile([P, D], F32, name="y_patch%d" % p) for p in range(PATCHES)]
+        bias_turned = keep.tile([P, COLUMN_BLOCKS], F32)
         x_class = keep.tile([P, P], BF16)
-        bias_class = keep.tile([P, P], BF16)
         y_class = keep.tile([P, P], F32)
         class_sums = keep.tile([P, P], F32)
+        class_means = keep.tile([P, P], F32)
 
         def patch_rows(dram, p):
             return dram[:, 1 + p * FRAMES : 1 + (p + 1) * FRAMES, :]
 
         def class_rows(dram):
-            return dram[:, 0, :].rearrange("b (c n) -> c b n", n=P)
+            return dram[:, 0, :].rearrange("b (c n) -> b c n", n=P)
 
         nc.vector.memset(bias_rows[:].bitcast(I32), 0)
         nc.vector.memset(ones[:], 1.0)
@@ -101,10 +106,6 @@ def tile_timesformerlayer_pc_kernel(tc, ctx_s, x_res, s_out_w, s_out_b, out):
         load_ctx(0)
         load_x(1)
         nc.sync.dma_start(out=x_class[:], in_=class_rows(x_res))
-        nc.sync.dma_start(
-            out=bias_class[:],
-            in_=s_out_b.rearrange("(c o n) -> c o n", o=1, n=P).to_broadcast([D // P, SAMPLES, P]),
-        )
         for c in range(1, len(ctx_chunks)):
             load_ctx(c)
             for p in range(c * CHUNK, min((c + 1) * CHUNK, PATCHES)):
@@ -113,27 +114,28 @@ def tile_timesformerlayer_pc_kernel(tc, ctx_s, x_res, s_out_w, s_out_b, out):
         nc.vector.tensor_copy(out=bias_rows[0:1, :], in_=bias_row[:])
         for h in range(HALVES):
             spread = psum_acc.tile([P, BANK], F32, tag="acc")
-            nc.tensor.matmul(out=spread[:], lhsT=ones[:], rhs=bias_rows[:, halves[h]], start=True, stop=True)
-            nc.scalar.copy(out=bias_all[:, halves[h]], in_=spread[:])
+            for target in (spread, bias_psum[h]):
+                nc.tensor.matmul(out=target[:], lhsT=ones[:], rhs=bias_rows[:, halves[h]], start=True, stop=True)
+            nc.scalar.copy(out=bias_sbuf[:, halves[h]], in_=spread[:])
+        bias_bank = psum_acc.tile([P, COLUMN_BLOCKS, P], BF16, tag="acc")
+        for c in range(COLUMN_BLOCKS):
+            nc.tensor.transpose(out=bias_bank[:, c, :], in_=bias_rows[:, c * P : (c + 1) * P], identity=ident_bf16[:])
 
         def add_bias(tokens):
-            for j in tokens:
-                p = j - 1
-                if j == 0:
-                    nc.vector.tensor_tensor(out=y_class[:], in0=x_class[:], in1=bias_class[:], op=ADD)
-                elif p % 3 == 0:
+            for p in [j - 1 for j in tokens if j > 0]:
+                if p % VECTOR_EVERY == VECTOR_EVERY - 1:
                     for h in range(HALVES):
-                        summed = psum_acc.tile([P, BANK], F32, tag="acc")
-                        nc.tensor.matmul(
-                            out=summed[:], lhsT=ident_bf16[:], rhs=x_patch[p][:, halves[h]], start=True, stop=False
+                        nc.vector.tensor_tensor(
+                            out=y_patch[p][:, halves[h]], in0=bias_psum[h][:], in1=x_patch[p][:, halves[h]], op=ADD
                         )
-                        nc.tensor.matmul(
-                            out=summed[:], lhsT=ones[:], rhs=bias_rows[:, halves[h]], start=False, stop=True
-                        )
-                        nc.scalar.copy(out=y_patch[p][:, halves[h]], in_=summed[:])
                 else:
-                    engine = nc.gpsimd if p % 3 == 1 else nc.vector
-                    engine.tensor_tensor(out=y_patch[p][:], in0=x_patch[p][:], in1=bias_all[:], op=ADD)
+                    for h in range(HALVES):
+                        nc.gpsimd.tensor_tensor(
+                            out=y_patch[p][:, halves[h]],
+                            in0=x_patch[p][:, halves[h]],
+                            in1=bias_sbuf[:, halves[h]],
+                            op=ADD,
+                        )
 
         def turn(tokens):
             grouped = work.tile([P, len(tokens) * D], BF16, align_bytes=64, tag="grouped")
@@ -198,7 +200,7 @@ def tile_timesformerlayer_pc_kernel(tc, ctx_s, x_res, s_out_w, s_out_b, out):
                 nc.vector.tensor_tensor(
                     out=y_patch[p][:, halves[h]], in0=banks[h][:], in1=y_patch[p][:, halves[h]], op=ADD
                 )
-                nc.sync.dma_start(out=patch_rows(out, p)[:, :, halves[h]], in_=y_patch[p][:, halves[h]])
+            nc.sync.dma_start(out=patch_rows(out, p), in_=y_patch[p][:])
 
         def multiply_class(codes, scales, i):
             banks = []
@@ -221,19 +223,27 @@ def tile_timesformerlayer_pc_kernel(tc, ctx_s, x_res, s_out_w, s_out_b, out):
             return banks
 
         def finish_class(banks):
-            per_bank = BANK // FRAMES
+            per_bank = BANK // P
             for h in range(HALVES):
                 nc.vector.tensor_reduce(
-                    out=class_sums[:, h * per_bank : (h + 1) * per_bank],
-                    in_=banks[h][:].rearrange("p (cb t) -> p cb t", t=FRAMES),
+                    out=class_sums[:].rearrange("p (b c) -> p c b", c=COLUMN_BLOCKS)[
+                        :, h * per_bank : (h + 1) * per_bank, :
+                    ],
+                    in_=banks[h][:].rearrange("p (c b t) -> p c b t", b=SAMPLES, t=FRAMES),
                     axis=mybir.AxisListType.X,
                     op=ADD,
                 )
-            back = psum_turn.tile([P, BLOCKS, P], F32, tag="turned")
-            nc.tensor.transpose(out=back[:, 0, :], in_=class_sums[:], identity=ident[:])
             nc.vector.scalar_tensor_tensor(
-                out=y_class[:], in0=back[:, 0, :], scalar=1.0 / FRAMES, in1=y_class[:], op0=MULT, op1=ADD
+                out=class_means[:].rearrange("p (b c) -> p b c", c=COLUMN_BLOCKS),
+                in0=class_sums[:].rearrange("p (b c) -> p b c", c=COLUMN_BLOCKS),
+                scalar=1.0 / FRAMES,
+                in1=bias_turned[:].unsqueeze(1).to_broadcast([P, SAMPLES, COLUMN_BLOCKS]),
+                op0=MULT,
+                op1=ADD,
             )
+            back = psum_turn.tile([P, BLOCKS, P], F32, tag="turned")
+            nc.tensor.transpose(out=back[:, 0, :], in_=class_means[:], identity=ident[:])
+            nc.vector.tensor_tensor(out=y_class[:], in0=back[:, 0, :], in1=x_class[:], op=ADD)
             nc.sync.dma_start(out=class_rows(out), in_=y_class[:])
 
         def multiply(tokens, codes, scales):
@@ -252,6 +262,7 @@ def tile_timesformerlayer_pc_kernel(tc, ctx_s, x_res, s_out_w, s_out_b, out):
         n_groups = len(token_groups)
         for g in range(PASSES):
             prepare_w(g)
+        nc.vector.tensor_copy(out=bias_turned[:], in_=bias_bank[:, :, 0])
         quantised = {}
         for u in range(2):
             quantised[u] = quantise(token_groups[u], turn(token_groups[u]))

from contextlib import ExitStack

import concourse.mybir as mybir
from concourse.masks import make_identity

F32 = mybir.dt.float32
BF16 = mybir.dt.bfloat16
I32 = mybir.dt.int32
U32 = mybir.dt.uint32
U8 = mybir.dt.uint8
FP8X4 = mybir.dt.float8_e4m3fn_x4
ADD = mybir.AluOpType.add
MULT = mybir.AluOpType.mult

P = 128
SAMPLES = 16
FRAMES = 8
PATCHES = 12
TOKENS = 1 + PATCHES
D = 1024
K_PASS = 512
PASSES = D // K_PASS
BANK = 512
HALVES = D // BANK
WORDS = D // 2
BLOCKS = WORDS // P
COLUMN_BLOCKS = D // P
CHUNK = 2
RUN = 4
W_VECTOR_COLS = 256
VECTOR_EVERY = 2

FLOPS = 2 * P * TOKENS * D * D


def tile_timesformerlayer_pc_kernel(tc, ctx_s, x_res, s_out_w, s_out_b, out):
    nc = tc.nc
    token_groups = [[0], [1]] + [[j, j + 1] for j in range(2, TOKENS - 1, 2)] + [[TOKENS - 1]]
    halves = [slice(h * BANK, (h + 1) * BANK) for h in range(HALVES)]

    with ExitStack() as stack:
        keep = stack.enter_context(tc.tile_pool(name="keep", bufs=1))
        work = stack.enter_context(tc.tile_pool(name="work", bufs=3))
        psum_bias = stack.enter_context(tc.psum_pool(name="psum_bias", bufs=1))
        psum_turn = stack.enter_context(tc.psum_pool(name="psum_turn", bufs=2))
        psum_acc = stack.enter_context(tc.psum_pool(name="psum_acc", bufs=4))
        stack.enter_context(tc.manual_schedule())

        ident = keep.tile([P, P], F32)
        ident_bf16 = keep.tile([P, P], BF16)
        ones = keep.tile([P, P], BF16)
        bias_row = keep.tile([1, D], BF16)
        bias_rows = keep.tile([P, D], BF16)
        bias_sbuf = keep.tile([P, D], F32)
        bias_psum = [psum_bias.tile([P, BANK], F32, name="bias_psum%d" % h) for h in range(HALVES)]
        ctx_chunks = [
            keep.tile([P, min(CHUNK, TOKENS - first) * D], BF16, name="ctx%d" % first)
            for first in range(0, TOKENS, CHUNK)
        ]
        w_raw = [keep.tile([P, 4, D], BF16, name="w_raw%d" % g) for g in range(PASSES)]
        w_grouped = [
            keep.tile([P, D, 4], BF16, name="w_grouped%d" % g, align_bytes=64) for g in range(PASSES)
        ]
        w_codes = [keep.tile([P, D], U32, name="w_codes%d" % g, align_bytes=64) for g in range(PASSES)]
        w_scales = [keep.tile([P, D], U8, name="w_scales%d" % g, align_bytes=64) for g in range(PASSES)]
        x_patch = [keep.tile([P, D], BF16, name="x_patch%d" % p) for p in range(PATCHES)]
        y_patch = [keep.tile([P, D], F32, name="y_patch%d" % p) for p in range(PATCHES)]
        bias_turned = keep.tile([P, COLUMN_BLOCKS], F32)
        x_class = keep.tile([P, P], BF16)
        y_class = keep.tile([P, P], F32)
        class_sums = keep.tile([P, P], F32)
        class_means = keep.tile([P, P], F32)

        def patch_rows(dram, p):
            return dram[:, 1 + p * FRAMES : 1 + (p + 1) * FRAMES, :]

        def class_rows(dram):
            return dram[:, 0, :].rearrange("b (c n) -> b c n", n=P)

        nc.vector.memset(bias_rows[:].bitcast(I32), 0)
        nc.vector.memset(ones[:], 1.0)
        make_identity(nc, ident[:])
        make_identity(nc, ident_bf16[:])

        def load_ctx(c):
            first = c * CHUNK
            last = min(first + CHUNK, TOKENS)
            nc.sync.dma_start(
                out=ctx_chunks[c][:], in_=ctx_s[:, first:last, :].rearrange("s j d -> s (j d)")
            )

        def load_w(g):
            rows = s_out_w[g * K_PASS : (g + 1) * K_PASS, :]
            nc.sync.dma_start(
                out=w_raw[g][:].rearrange("p (u e) n -> p u (e n)", e=2),
                in_=rows.rearrange("(u p e) n -> p u (e n)", u=2, e=2),
            )

        def load_x(p):
            nc.sync.dma_start(out=x_patch[p][:], in_=patch_rows(x_res, p))

        nc.sync.dma_start(out=bias_row[:], in_=s_out_b.rearrange("(o n) -> o n", o=1))
        load_w(0)
        load_x(0)
        load_w(1)
        load_ctx(0)
        load_x(1)
        nc.sync.dma_start(out=x_class[:], in_=class_rows(x_res))
        for c in range(1, len(ctx_chunks)):
            load_ctx(c)
            for p in range(c * CHUNK, min((c + 1) * CHUNK, PATCHES)):
                load_x(p)

        nc.vector.tensor_copy(out=bias_rows[0:1, :], in_=bias_row[:])
        for h in range(HALVES):
            spread = psum_acc.tile([P, BANK], F32, tag="acc")
            for target in (spread, bias_psum[h]):
                nc.tensor.matmul(out=target[:], lhsT=ones[:], rhs=bias_rows[:, halves[h]], start=True, stop=True)
            nc.scalar.copy(out=bias_sbuf[:, halves[h]], in_=spread[:])
        bias_bank = psum_acc.tile([P, COLUMN_BLOCKS, P], BF16, tag="acc")
        for c in range(COLUMN_BLOCKS):
            nc.tensor.transpose(out=bias_bank[:, c, :], in_=bias_rows[:, c * P : (c + 1) * P], identity=ident_bf16[:])

        def add_bias(tokens):
            for p in [j - 1 for j in tokens if j > 0]:
                if p % VECTOR_EVERY == VECTOR_EVERY - 1:
                    for h in range(HALVES):
                        nc.vector.tensor_tensor(
                            out=y_patch[p][:, halves[h]], in0=bias_psum[h][:], in1=x_patch[p][:, halves[h]], op=ADD
                        )
                else:
                    for h in range(HALVES):
                        nc.gpsimd.tensor_tensor(
                            out=y_patch[p][:, halves[h]],
                            in0=x_patch[p][:, halves[h]],
                            in1=bias_sbuf[:, halves[h]],
                            op=ADD,
                        )

        def turn(tokens):
            grouped = work.tile([P, len(tokens) * D], BF16, align_bytes=64, tag="grouped")
            grouped_words = grouped[:].bitcast(F32)
            for i, j in enumerate(tokens):
                words = ctx_chunks[j // CHUNK][:].bitcast(F32)
                turned = psum_turn.tile([P, BLOCKS, P], F32, tag="turned")
                for blk in range(BLOCKS):
                    first = (j % CHUNK) * WORDS + blk * P
                    nc.tensor.transpose(out=turned[:, blk, :], in_=words[:, first : first + P], identity=ident[:])
                nc.scalar.copy(
                    out=grouped_words[:, i * WORDS : (i + 1) * WORDS].rearrange(
                        "p (g r u) -> p g r u", g=PASSES, u=2
                    ),
                    in_=turned[:].rearrange("p (g u) r -> p g r u", u=2),
                )
            return grouped

        def quantise(tokens, grouped):
            codes = work.tile([P, len(tokens) * PASSES * P], U32, align_bytes=64, tag="codes")
            scales = work.tile([P, len(tokens) * PASSES * P], U8, align_bytes=64, tag="scales")
            nc.vector.quantize_mx(out=codes[:].bitcast(FP8X4), scales=scales[:], in_=grouped[:])
            return codes, scales

        def regroup_w(copy, g, first, last):
            copy(
                out=w_grouped[g][:, first:last, :].rearrange("p (c i) t -> p c t i", i=RUN),
                in_=w_raw[g][:, :, first:last].rearrange("p t (c i) -> p c t i", i=RUN),
            )

        def prepare_w(g):
            for h in range(HALVES):
                regroup_w(nc.vector.tensor_copy, g, h * BANK, h * BANK + W_VECTOR_COLS)
                regroup_w(nc.scalar.copy, g, h * BANK + W_VECTOR_COLS, (h + 1) * BANK)
            for h in range(HALVES):
                nc.vector.quantize_mx(
                    out=w_codes[g][:, halves[h]].bitcast(FP8X4),
                    scales=w_scales[g][:, halves[h]],
                    in_=w_grouped[g][:, halves[h], :].rearrange("p n t -> p (n t)"),
                )

        def multiply_patch(codes, scales, i):
            banks = []
            for h in range(HALVES):
                acc = psum_acc.tile([P, BANK], F32, tag="acc")
                for g in range(PASSES):
                    rows = slice((i * PASSES + g) * P, (i * PASSES + g + 1) * P)
                    nc.tensor.matmul_mx(
                        out=acc[:],
                        lhsT=codes[:, rows].bitcast(FP8X4),
                        lhsT_scale=scales[:, rows],
                        rhs=w_codes[g][:, halves[h]].bitcast(FP8X4),
                        rhs_scale=w_scales[g][:, halves[h]],
                        start=(g == 0),
                        stop=(g == PASSES - 1),
                    )
                banks.append(acc)
            return banks

        def finish_patch(p, banks):
            for h in range(HALVES):
                nc.vector.tensor_tensor(
                    out=y_patch[p][:, halves[h]], in0=banks[h][:], in1=y_patch[p][:, halves[h]], op=ADD
                )
            nc.sync.dma_start(out=patch_rows(out, p), in_=y_patch[p][:])

        def multiply_class(codes, scales, i):
            banks = []
            for h in range(HALVES):
                acc = psum_acc.tile([P, BANK], F32, tag="acc")
                for q in range(BANK // P):
                    cols = slice(h * BANK + q * P, h * BANK + (q + 1) * P)
                    for g in range(PASSES):
                        rows = slice((i * PASSES + g) * P, (i * PASSES + g + 1) * P)
                        nc.tensor.matmul_mx(
                            out=acc[:, q * P : (q + 1) * P],
                            lhsT=w_codes[g][:, cols].bitcast(FP8X4),
                            lhsT_scale=w_scales[g][:, cols],
                            rhs=codes[:, rows].bitcast(FP8X4),
                            rhs_scale=scales[:, rows],
                            start=(g == 0),
                            stop=(g == PASSES - 1),
                        )
                banks.append(acc)
            return banks

        def finish_class(banks):
            per_bank = BANK // P
            for h in range(HALVES):
                nc.vector.tensor_reduce(
                    out=class_sums[:].rearrange("p (b c) -> p c b", c=COLUMN_BLOCKS)[
                        :, h * per_bank : (h + 1) * per_bank, :
                    ],
                    in_=banks[h][:].rearrange("p (c b t) -> p c b t", b=SAMPLES, t=FRAMES),
                    axis=mybir.AxisListType.X,
                    op=ADD,
                )
            nc.vector.scalar_tensor_tensor(
                out=class_means[:].rearrange("p (b c) -> p b c", c=COLUMN_BLOCKS),
                in0=class_sums[:].rearrange("p (b c) -> p b c", c=COLUMN_BLOCKS),
                scalar=1.0 / FRAMES,
                in1=bias_turned[:].unsqueeze(1).to_broadcast([P, SAMPLES, COLUMN_BLOCKS]),
                op0=MULT,
                op1=ADD,
            )
            back = psum_turn.tile([P, BLOCKS, P], F32, tag="turned")
            nc.tensor.transpose(out=back[:, 0, :], in_=class_means[:], identity=ident[:])
            nc.vector.tensor_tensor(out=y_class[:], in0=back[:, 0, :], in1=x_class[:], op=ADD)
            nc.sync.dma_start(out=class_rows(out), in_=y_class[:])

        def multiply(tokens, codes, scales):
            return [
                multiply_class(codes, scales, i) if j == 0 else multiply_patch(codes, scales, i)
                for i, j in enumerate(tokens)
            ]

        def finish(tokens, banks):
            for i, j in enumerate(tokens):
                if j == 0:
                    finish_class(banks[i])
                else:
                    finish_patch(j - 1, banks[i])

        n_groups = len(token_groups)
        for g in range(PASSES):
            prepare_w(g)
        nc.vector.tensor_copy(out=bias_turned[:], in_=bias_bank[:, :, 0])
        quantised = {}
        for u in range(2):
            quantised[u] = quantise(token_groups[u], turn(token_groups[u]))
            add_bias(token_groups[u])
        for u in range(n_groups):
            codes, scales = quantised[u]
            banks = multiply(token_groups[u], codes, scales)
            if u + 2 < n_groups:
                grouped = turn(token_groups[u + 2])
                add_bias(token_groups[u + 2])
            finish(token_groups[u], banks)
            if u + 2 < n_groups:
                quantised[u + 2] = quantise(token_groups[u + 2], grouped)
